import numpy as np
import ml_dtypes


def mxq(x, axis, fmt="e4m3"):
    dtype, down = {"e4m3": (ml_dtypes.float8_e4m3fn, 7), "e5m2": (ml_dtypes.float8_e5m2, 14)}[fmt]
    v = np.moveaxis(np.asarray(x, np.float32).astype(ml_dtypes.bfloat16).astype(np.float64), axis, -1)
    blocks = v.reshape(v.shape[:-1] + (-1, 32))
    amax = np.abs(blocks).max(-1, keepdims=True)
    byte = np.maximum(np.where(amax > 0, np.frexp(amax)[1] - 1 + 127, 0) - down, 1)
    scale = np.exp2(byte - 127.0)
    codes = (blocks / scale).astype(np.float32).astype(dtype).astype(np.float64)
    return np.moveaxis((codes * scale).reshape(v.shape), -1, axis)


WIDE = False


def mx_kscale(k):
    if not WIDE:
        return np.ones(k)
    levels = np.array([10, -10, 5, -5, 0])
    a = np.random.permutation(np.resize(levels, k // 512 * 4)).reshape(k // 512, 4)
    idx = np.arange(k)
    return np.exp2(a[idx // 512, idx % 128 // 32])


BF16 = ml_dtypes.bfloat16


def bf(x):
    return np.asarray(x, np.float32).astype(BF16)


def f64(x):
    return np.asarray(x).astype(np.float64)


B, N, C, O = 4, 512, 1024, 1024


def setup_inputs():
    t = mx_kscale(C)
    strength = (0.2 + 1.8 * np.random.random((B, N, 1))) * (np.random.random((B, N, 1)) >= 0.1)
    adj = np.random.random((B, N, N)) * strength * 50.0 / N
    feat = np.random.standard_normal((B, N, C)) * 3.0 * t
    return {"X": bf(np.concatenate([adj, feat], axis=2)), "W": bf(np.random.standard_normal((C, O)) * 3.0 / np.sqrt(C) / t[:, None])}


def reference(X, W):
    X = f64(X)
    A = X[:, :, :N]
    feat = X[:, :, N:]
    deg = A.sum(axis=2)
    d_inv_sqrt = np.where(deg > 0, 1.0 / np.sqrt(np.where(deg > 0, deg, 1.0)), 0.0)
    A_hat = A + np.eye(N)
    A_norm = d_inv_sqrt[:, :, None] * A_hat * d_inv_sqrt[:, None, :]
    h = mxq(A_norm, 2, "e4m3") @ mxq(feat, 1, "e4m3")
    return np.maximum(mxq(h, 2, "e4m3") @ mxq(f64(W), 0, "e4m3"), 0.0)

@@ -1,0 +1,536 @@
+from contextlib import ExitStack
+
+import concourse.mybir as mybir
+from concourse.masks import make_identity
+
+FLOPS = 2 * 4 * 512 * 512 * 1024 + 2 * 4 * 512 * 1024 * 1024
+
+FP8X4 = mybir.dt.float8_e4m3fn_x4
+BF16 = mybir.dt.bfloat16
+F32 = mybir.dt.float32
+U32 = mybir.dt.uint32
+U8 = mybir.dt.uint8
+ALU = mybir.AluOpType
+ACT = mybir.ActivationFunctionType
+AXIS = mybir.AxisListType
+
+P = 128
+B, N, C, O = 4, 512, 1024, 1024
+HB = 8
+
+
+def tile_gcnconv_pa_kernel(tc, X, W, out):
+    nc = tc.nc
+    with ExitStack() as ctx:
+        keep = ctx.enter_context(tc.tile_pool(name="keep", bufs=1))
+        rot = ctx.enter_context(tc.tile_pool(name="rot", bufs=2))
+        psum = ctx.enter_context(tc.psum_pool(name="psum", bufs=2))
+        ctx.enter_context(tc.manual_schedule())
+
+        ident_bf = keep.tile([P, P], BF16, name="ident_bf")
+        ident_f = keep.tile([P, P], F32, name="ident_f")
+        warm = keep.tile([P, 1], F32, name="warm")
+        junk = keep.tile([P, N], BF16, name="junk")
+        xs = [keep.tile([P, 4, N + C], BF16, name="xs%d" % b) for b in range(B)]
+        ws = keep.tile([P, 8, O], BF16, name="ws")
+        wg = keep.tile([P, 2, O, 4], BF16, name="wg", align_bytes=64)
+        wc = keep.tile([P, 2, O], U32, name="wc", align_bytes=64)
+        wsc = keep.tile([P, 2, O], U8, name="wsc", align_bytes=64)
+        T = {}
+
+        Xv = X.rearrange("b (t p) w -> b p t w", p=P)
+        Wv = W.rearrange("(g p) o -> p g o", p=P)
+
+        def ld_x(b, lo, hi):
+            nc.sync.dma_start(out=xs[b][:, :, lo:hi], in_=Xv[b][:, :, lo:hi])
+
+        def ld_w(g):
+            nc.sync.dma_start(out=ws[:, 4 * g:4 * g + 4, :], in_=Wv[:, 4 * g:4 * g + 4, :])
+
+        def copy_on(eng, dst, src):
+            if eng == "V":
+                nc.vector.tensor_copy(out=dst, in_=src)
+            else:
+                nc.scalar.copy(out=dst, in_=src)
+
+        def regroup(eng, dst, src):
+            copy_on(eng, dst.rearrange("p (c i) t -> p c t i", i=4), src.rearrange("p t (c i) -> p c t i", i=4))
+
+        def deg_tiles(b):
+            T["deg", b] = rot.tile([P, 2, 8], F32, name="deg", bufs=4)
+
+        def deg_s(b, t):
+            nc.scalar.activation(out=junk[:], in_=xs[b][:, t, 0:N], func=ACT.Copy,
+                                 accum_out=T["deg", b][:, t // 2, t % 2:t % 2 + 1])
+
+        def deg_v(b, h):
+            nc.vector.tensor_reduce(out=T["deg", b][:, h, 0:2], in_=xs[b][:, 2 * h:2 * h + 2, 0:N], axis=AXIS.X, op=ALU.add)
+
+        def deg(b, h, eng):
+            if eng == "V":
+                deg_v(b, h)
+            else:
+                deg_s(b, 2 * h)
+                deg_s(b, 2 * h + 1)
+
+        def ch1(b):
+            safe = rot.tile([P, 2, 2], F32, name="safe", bufs=4)
+            T["safe", b] = safe
+            dg = T["deg", b][:, :, 0:2]
+            nc.vector.scalar_tensor_tensor(out=safe[:], in0=dg, scalar=0.0, in1=dg, op0=ALU.is_le, op1=ALU.max)
+
+        def ch2(b):
+            sq = rot.tile([P, 2, 2], F32, name="sq", bufs=4)
+            T["sq", b] = sq
+            nc.scalar.activation(out=sq[:], in_=T["safe", b][:], func=ACT.Sqrt)
+
+        def ch3(b):
+            rc = rot.tile([P, 2, 2], F32, name="rc", bufs=4)
+            d = rot.tile([P, 4], F32, name="d", bufs=4)
+            T["d", b] = d
+            nc.vector.reciprocal(out=rc[:], in_=T["sq", b][:])
+            nc.vector.scalar_tensor_tensor(out=d[:].rearrange("p (h c) -> p h c", c=2), in0=T["deg", b][:, :, 0:2], scalar=0.0,
+                                           in1=rc[:], op0=ALU.is_gt, op1=ALU.mult)
+
+        def db(b):
+            pdb = psum.tile([P, N], F32, name="pt")
+            T["pdb", b] = pdb
+            for t in range(4):
+                nc.tensor.matmul(out=pdb[:, t * P:(t + 1) * P], lhsT=T["d", b][:, t:t + 1].to_broadcast([P, P]), rhs=ident_f[:],
+                                 start=True, stop=True)
+
+        def dbc(b):
+            t_ = rot.tile([P, N], F32, name="dbc", bufs=4)
+            T["dbc", b] = t_
+            nc.scalar.copy(out=t_[:], in_=T["pdb", b][:])
+
+        def f_tile(b):
+            T["F", b] = rot.tile([P, 4, N], F32, name="F")
+
+        def f_v(b, t):
+            nc.vector.tensor_scalar(out=T["F", b][:, t, :], in0=T["dbc", b][:], scalar1=T["d", b][:, t:t + 1], scalar2=None, op0=ALU.mult)
+
+        def f_s(b, t):
+            nc.scalar.activation(out=T["F", b][:, t, :], in_=T["pdb", b][:], func=ACT.Copy, scale=T["d", b][:, t:t + 1])
+
+        def tm(b, r):
+            pat = psum.tile([P, 4, P], F32, name="pt")
+            T["pat", b, r] = pat
+            for t in range(4):
+                nc.tensor.matmul(out=pat[:, t, :], lhsT=xs[b][:, r, t * P:(t + 1) * P], rhs=ident_bf[:], start=True, stop=(t != r))
+                if t == r:
+                    nc.tensor.matmul(out=pat[:, t, :], lhsT=ident_bf[:], rhs=ident_bf[:], start=False, stop=True)
+
+        def a_tiles(b):
+            T["ag", b] = rot.tile([P, 4, P, 4], BF16, name="ag", bufs=4, align_bytes=64)
+            T["ac", b] = rot.tile([P, N], U32, name="ac", bufs=4, align_bytes=64)
+            T["as", b] = rot.tile([P, N], U8, name="as", bufs=4, align_bytes=64)
+
+        def ax(b, r):
+            nc.vector.tensor_tensor(out=T["ag", b][:, r, :, :], in0=T["pat", b, r][:].rearrange("p t n -> p n t"),
+                                    in1=T["F", b][:, :, r * P:(r + 1) * P].rearrange("p t n -> p n t"), op=ALU.mult)
+
+        def aq(b, r0, nr):
+            cols = slice(r0 * P, (r0 + nr) * P)
+            nc.vector.quantize_mx(out=T["ac", b][:, cols].bitcast(FP8X4), scales=T["as", b][:, cols],
+                                  in_=T["ag", b][:, r0:r0 + nr, :, :].rearrange("p r n t -> p (r n t)"))
+
+        def f_tiles(b):
+            T["fg", b] = rot.tile([P, C, 4], BF16, name="fg", align_bytes=64)
+            T["fc", b] = rot.tile([P, C], U32, name="fc", bufs=4, align_bytes=64)
+            T["fs", b] = rot.tile([P, C], U8, name="fs", bufs=4, align_bytes=64)
+
+        def fr(b, c0, c1, eng):
+            regroup(eng, T["fg", b][:, c0:c1, :], xs[b][:, :, N + c0:N + c1])
+
+        def fq(b, c0, c1):
+            nc.vector.quantize_mx(out=T["fc", b][:, c0:c1].bitcast(FP8X4), scales=T["fs", b][:, c0:c1],
+                                  in_=T["fg", b][:, c0:c1, :].rearrange("p c t -> p (c t)"))
+
+        def wr(g, o0, o1, eng):
+            regroup(eng, wg[:, g, o0:o1, :], ws[:, 4 * g:4 * g + 4, o0:o1])
+
+        def wq(g, o0, o1):
+            nc.vector.quantize_mx(out=wc[:, g, o0:o1].bitcast(FP8X4), scales=wsc[:, g, o0:o1],
+                                  in_=wg[:, g, o0:o1, :].rearrange("p o t -> p (o t)"))
+
+        def h_tiles(b, r):
+            T["hg", b, r] = rot.tile([P, 2, P, 4], BF16, name="hg", bufs=HB, align_bytes=64)
+            T["hc", b, r] = rot.tile([P, 2 * P], U32, name="hc", bufs=HB, align_bytes=64)
+            T["hs", b, r] = rot.tile([P, 2 * P], U8, name="hs", bufs=HB, align_bytes=64)
+
+        def o_tile(b, r):
+            T["ost", b, r] = rot.tile([P, O], F32, name="ost", bufs=4)
+
+        def m1(b, r, g):
+            ph = psum.tile([P, 4, P], F32, name="ph", bufs=4)
+            T["ph", b, r, g] = ph
+            ncol = slice(r * P, (r + 1) * P)
+            for t in range(4):
+                ccol = slice((4 * g + t) * P, (4 * g + t + 1) * P)
+                nc.tensor.matmul_mx(out=ph[:, t, :], lhsT=T["fc", b][:, ccol].bitcast(FP8X4), lhsT_scale=T["fs", b][:, ccol],
+                                    rhs=T["ac", b][:, ncol].bitcast(FP8X4), rhs_scale=T["as", b][:, ncol], start=True, stop=True)
+
+        def hx(b, r, g, eng):
+            copy_on(eng, T["hg", b, r][:, g, :, :], T["ph", b, r, g][:].rearrange("p t n -> p n t"))
+
+        def hq(b, r):
+            nc.vector.quantize_mx(out=T["hc", b, r][:].bitcast(FP8X4), scales=T["hs", b, r][:],
+                                  in_=T["hg", b, r][:].rearrange("p g n t -> p (g n t)"))
+
+        def m2(b, r, oh):
+            po = psum.tile([P, 512], F32, name="po")
+            T["po", b, r, oh] = po
+            ocol = slice(oh * 512, (oh + 1) * 512)
+            for g in range(2):
+                ncol = slice(g * P, (g + 1) * P)
+                nc.tensor.matmul_mx(out=po[:], lhsT=T["hc", b, r][:, ncol].bitcast(FP8X4), lhsT_scale=T["hs", b, r][:, ncol],
+                                    rhs=wc[:, g, ocol].bitcast(FP8X4), rhs_scale=wsc[:, g, ocol], start=(g == 0), stop=(g == 1))
+
+        def ox(b, r, oh, eng):
+            dst = T["ost", b, r][:, oh * 512:(oh + 1) * 512]
+            if eng == "V":
+                nc.vector.tensor_scalar_max(out=dst, in0=T["po", b, r, oh][:], scalar1=0.0)
+            else:
+                nc.scalar.activation(out=dst, in_=T["po", b, r, oh][:], func=ACT.Relu)
+
+        def st(b, r):
+            nc.sync.dma_start(out=out[b, r * P:(r + 1) * P, :], in_=T["ost", b, r][:])
+
+        make_identity(nc, ident_bf[:])
+        make_identity(nc, ident_f[:])
+        nc.vector.memset(warm[:], 1.0)
+        nc.scalar.activation(out=warm[:], in_=warm[:], func=ACT.Sqrt)
+        ld_x(0, 0, N)
+        ld_x(0, N, N + C)
+        deg_tiles(0)
+        deg(0, 0, "S")
+        deg(0, 1, "V")
+        ld_w(0)
+        ch1(0)
+        ch2(0)
+        ch3(0)
+        db(0)
+        f_tiles(0)
+        fr(0, 0, 256, "S")
+        fr(0, 256, 512, "V")
+        ld_w(1)
+        tm(0, 0)
+        fr(0, 512, 768, "V")
+        dbc(0)
+        fr(0, 768, 1024, "V")
+        tm(0, 1)
+        f_tile(0)
+        f_v(0, 0)
+        f_v(0, 1)
+        wr(0, 0, 512, "S")
+        f_v(0, 2)
+        ld_x(1, 0, N + C)
+        f_v(0, 3)
+        fq(0, 0, 512)
+        a_tiles(0)
+        ax(0, 0)
+        fq(0, 512, 1024)
+        tm(0, 2)
+        wr(0, 512, 1024, "S")
+        aq(0, 0, 1)
+        wr(1, 0, 512, "V")
+        h_tiles(0, 0)
+        m1(0, 0, 0)
+        m1(0, 0, 1)
+        ld_x(2, 0, N + C)
+        wr(1, 512, 1024, "V")
+        hx(0, 0, 0, "S")
+        hx(0, 0, 1, "S")
+        ax(0, 1)
+        wq(0, 0, 512)
+        tm(0, 3)
+        deg_tiles(1)
+        deg(1, 0, "S")
+        wq(1, 0, 512)
+        aq(0, 1, 1)
+        hq(0, 0)
+        deg(1, 1, "S")
+        h_tiles(0, 1)
+        m1(0, 1, 0)
+        ld_x(3, 0, N + C)
+        wq(0, 512, 1024)
+        m2(0, 0, 0)
+        wq(1, 512, 1024)
+        m1(0, 1, 1)
+        ax(0, 2)
+        hx(0, 1, 0, "S")
+        m2(0, 0, 1)
+        ch1(1)
+        hx(0, 1, 1, "S")
+        aq(0, 2, 1)
+        o_tile(0, 0)
+        ox(0, 0, 0, "V")
+        h_tiles(0, 2)
+        m1(0, 2, 0)
+        ch2(1)
+        ox(0, 0, 1, "S")
+        m1(0, 2, 1)
+        hq(0, 1)
+        ch3(1)
+        ax(0, 3)
+        hx(0, 2, 0, "S")
+        db(1)
+        st(0, 0)
+        f_tiles(1)
+        fr(1, 0, 256, "V")
+        hx(0, 2, 1, "S")
+        m2(0, 1, 0)
+        deg_tiles(2)
+        deg(2, 0, "S")
+        aq(0, 3, 1)
+        hq(0, 2)
+        fr(1, 256, 512, "V")
+        m2(0, 1, 1)
+        tm(1, 0)
+        fr(1, 512, 768, "V")
+        dbc(1)
+        h_tiles(0, 3)
+        m1(0, 3, 0)
+        m1(0, 3, 1)
+        fr(1, 768, 1024, "V")
+        o_tile(0, 1)
+        ox(0, 1, 0, "S")
+        tm(1, 1)
+        f_tile(1)
+        f_v(1, 0)
+        ox(0, 1, 1, "S")
+        m2(0, 2, 0)
+        f_v(1, 1)
+        f_v(1, 2)
+        hx(0, 3, 0, "S")
+        m2(0, 2, 1)
+        st(0, 1)
+        f_v(1, 3)
+        hx(0, 3, 1, "S")
+        fq(1, 0, 512)
+        o_tile(0, 2)
+        ox(0, 2, 0, "S")
+        a_tiles(1)
+        ax(1, 0)
+        ox(0, 2, 1, "S")
+        ax(1, 1)
+        tm(1, 2)
+        deg(2, 1, "S")
+        st(0, 2)
+        fq(1, 512, 1024)
+        tm(1, 3)
+        aq(1, 0, 2)
+        hq(0, 3)
+        h_tiles(1, 0)
+        m1(1, 0, 0)
+        ax(1, 2)
+        deg_tiles(3)
+        deg(3, 0, "S")
+        m2(0, 3, 0)
+        hx(1, 0, 0, "V")
+        m1(1, 0, 1)
+        m2(0, 3, 1)
+        ax(1, 3)
+        hx(1, 0, 1, "S")
+        h_tiles(1, 1)
+        m1(1, 1, 0)
+        ch1(2)
+        aq(1, 2, 2)
+        o_tile(0, 3)
+        ox(0, 3, 0, "S")
+        m1(1, 1, 1)
+        hq(1, 0)
+        h_tiles(1, 2)
+        m1(1, 2, 0)
+        f_tiles(2)
+        fr(2, 0, 256, "V")
+        ox(0, 3, 1, "S")
+        m2(1, 0, 0)
+        fr(2, 256, 512, "V")
+        hx(1, 1, 0, "S")
+        st(0, 3)
+        m2(1, 0, 1)
+        hx(1, 1, 1, "S")
+        o_tile(1, 0)
+        ox(1, 0, 0, "V")
+        m1(1, 2, 1)
+        h_tiles(1, 3)
+        m1(1, 3, 0)
+        ch2(2)
+        fr(2, 512, 768, "V")
+        ox(1, 0, 1, "S")
+        m1(1, 3, 1)
+        hx(1, 2, 0, "S")
+        hq(1, 1)
+        st(1, 0)
+        ch3(2)
+        fr(2, 768, 1024, "V")
+        db(2)
+        hx(1, 2, 1, "S")
+        fq(2, 0, 512)
+        hx(1, 3, 0, "S")
+        m2(1, 1, 0)
+        hq(1, 2)
+        hx(1, 3, 1, "S")
+        fq(2, 512, 1024)
+        m2(1, 1, 1)
+        dbc(2)
+        o_tile(1, 1)
+        ox(1, 1, 0, "V")
+        tm(2, 0)
+        ox(1, 1, 1, "S")
+        tm(2, 1)
+        f_tile(2)
+        f_v(2, 0)
+        m2(1, 2, 0)
+        f_v(2, 1)
+        deg(3, 1, "S")
+        st(1, 1)
+        f_v(2, 2)
+        m2(1, 2, 1)
+        f_v(2, 3)
+        hq(1, 3)
+        a_tiles(2)
+        ax(2, 0)
+        o_tile(1, 2)
+        ox(1, 2, 0, "S")
+        ax(2, 1)
+        ox(1, 2, 1, "S")
+        tm(2, 2)
+        m2(1, 3, 0)
+        ch1(3)
+        aq(2, 0, 2)
+        st(1, 2)
+        ch2(3)
+        ax(2, 2)
+        m2(1, 3, 1)
+        o_tile(1, 3)
+        ox(1, 3, 0, "S")
+        h_tiles(2, 0)
+        m1(2, 0, 0)
+        ch3(3)
+        f_tiles(3)
+        fr(3, 0, 256, "V")
+        ox(1, 3, 1, "S")
+        m1(2, 0, 1)
+        tm(2, 3)
+        fr(3, 256, 512, "V")
+        hx(2, 0, 0, "S")
+        st(1, 3)
+        h_tiles(2, 1)
+        m1(2, 1, 0)
+        m1(2, 1, 1)
+        hx(2, 0, 1, "S")
+        ax(2, 3)
+        db(3)
+        hx(2, 1, 0, "S")
+        hq(2, 0)
+        aq(2, 2, 2)
+        hx(2, 1, 1, "S")
+        m2(2, 0, 0)
+        fr(3, 512, 768, "V")
+        dbc(3)
+        m2(2, 0, 1)
+        hq(2, 1)
+        fr(3, 768, 1024, "V")
+        o_tile(2, 0)
+        ox(2, 0, 0, "S")
+        h_tiles(2, 2)
+        m1(2, 2, 0)
+        m1(2, 2, 1)
+        f_tile(3)
+        f_v(3, 0)
+        ox(2, 0, 1, "S")
+        tm(3, 0)
+        f_v(3, 1)
+        m2(2, 1, 0)
+        f_v(3, 2)
+        hx(2, 2, 0, "S")
+        st(2, 0)
+        f_v(3, 3)
+        m2(2, 1, 1)
+        hx(2, 2, 1, "S")
+        o_tile(2, 1)
+        ox(2, 1, 0, "V")
+        tm(3, 1)
+        ox(2, 1, 1, "S")
+        hq(2, 2)
+        h_tiles(2, 3)
+        m1(2, 3, 0)
+        a_tiles(3)
+        ax(3, 0)
+        m1(2, 3, 1)
+        hx(2, 3, 0, "S")
+        st(2, 1)
+        m2(2, 2, 0)
+        ax(3, 1)
+        hx(2, 3, 1, "S")
+        m2(2, 2, 1)
+        fq(3, 0, 512)
+        o_tile(2, 2)
+        ox(2, 2, 0, "S")
+        tm(3, 2)
+        aq(3, 0, 2)
+        tm(3, 3)
+        ox(2, 2, 1, "S")
+        fq(3, 512, 1024)
+        h_tiles(3, 0)
+        m1(3, 0, 0)
+        hq(2, 3)
+        st(2, 2)
+        hx(3, 0, 0, "S")
+        m1(3, 0, 1)
+        ax(3, 2)
+        m2(2, 3, 0)
+        hx(3, 0, 1, "S")
+        ax(3, 3)
+        m2(2, 3, 1)
+        o_tile(2, 3)
+        ox(2, 3, 0, "S")
+        hq(3, 0)
+        h_tiles(3, 1)
+        m1(3, 1, 0)
+        aq(3, 2, 2)
+        ox(2, 3, 1, "S")
+        m1(3, 1, 1)
+        m2(3, 0, 0)
+        hx(3, 1, 1, "V")
+        hx(3, 1, 0, "S")
+        st(2, 3)
+        m2(3, 0, 1)
+        o_tile(3, 0)
+        ox(3, 0, 0, "S")
+        hq(3, 1)
+        h_tiles(3, 2)
+        m1(3, 2, 0)
+        m1(3, 2, 1)
+        ox(3, 0, 1, "S")
+        hx(3, 2, 0, "V")
+        m2(3, 1, 0)
+        hx(3, 2, 1, "S")
+        st(3, 0)
+        m2(3, 1, 1)
+        o_tile(3, 1)
+        ox(3, 1, 0, "S")
+        hq(3, 2)
+        h_tiles(3, 3)
+        m1(3, 3, 0)
+        m1(3, 3, 1)
+        ox(3, 1, 1, "S")
+        hx(3, 3, 0, "V")
+        m2(3, 2, 0)
+        hx(3, 3, 1, "S")
+        st(3, 1)
+        m2(3, 2, 1)
+        o_tile(3, 2)
+        ox(3, 2, 0, "S")
+        hq(3, 3)
+        ox(3, 2, 1, "S")
+        m2(3, 3, 0)
+        m2(3, 3, 1)
+        st(3, 2)
+        o_tile(3, 3)
+        ox(3, 3, 0, "S")
+        ox(3, 3, 1, "S")
+        st(3, 3)

@@ -17,6 +17,8 @@ AXIS = mybir.AxisListType
 P = 128
 B, N, C, O = 4, 512, 1024, 1024
 HB = 8
+PTB = 3
+PHB = 3
 
 
 def tile_gcnconv_pa_kernel(tc, X, W, out):
@@ -93,7 +95,7 @@ def tile_gcnconv_pa_kernel(tc, X, W, out):
                                            in1=rc[:], op0=ALU.is_gt, op1=ALU.mult)
 
         def db(b):
-            pdb = psum.tile([P, N], F32, name="pt")
+            pdb = psum.tile([P, N], F32, name="bank", bufs=8)
             T["pdb", b] = pdb
             for t in range(4):
                 nc.tensor.matmul(out=pdb[:, t * P:(t + 1) * P], lhsT=T["d", b][:, t:t + 1].to_broadcast([P, P]), rhs=ident_f[:],
@@ -114,7 +116,7 @@ def tile_gcnconv_pa_kernel(tc, X, W, out):
             nc.scalar.activation(out=T["F", b][:, t, :], in_=T["pdb", b][:], func=ACT.Copy, scale=T["d", b][:, t:t + 1])
 
         def tm(b, r):
-            pat = psum.tile([P, 4, P], F32, name="pt")
+            pat = psum.tile([P, 4, P], F32, name="bank", bufs=8)
             T["pat", b, r] = pat
             for t in range(4):
                 nc.tensor.matmul(out=pat[:, t, :], lhsT=xs[b][:, r, t * P:(t + 1) * P], rhs=ident_bf[:], start=True, stop=(t != r))
@@ -163,7 +165,7 @@ def tile_gcnconv_pa_kernel(tc, X, W, out):
             T["ost", b, r] = rot.tile([P, O], F32, name="ost", bufs=4)
 
         def m1(b, r, g):
-            ph = psum.tile([P, 4, P], F32, name="ph", bufs=4)
+            ph = psum.tile([P, 4, P], F32, name="bank", bufs=8)
             T["ph", b, r, g] = ph
             ncol = slice(r * P, (r + 1) * P)
             for t in range(4):
@@ -179,7 +181,7 @@ def tile_gcnconv_pa_kernel(tc, X, W, out):
                                   in_=T["hg", b, r][:].rearrange("p g n t -> p (g n t)"))
 
         def m2(b, r, oh):
-            po = psum.tile([P, 512], F32, name="po")
+            po = psum.tile([P, 512], F32, name="bank", bufs=8)
             T["po", b, r, oh] = po
             ocol = slice(oh * 512, (oh + 1) * 512)
             for g in range(2):
@@ -197,340 +199,138 @@ def tile_gcnconv_pa_kernel(tc, X, W, out):
         def st(b, r):
             nc.sync.dma_start(out=out[b, r * P:(r + 1) * P, :], in_=T["ost", b, r][:])
 
+        LAG = 2
+        def EX(i):
+            return (["S", "S", "S", "V" if (i % 4 < 2) else "S"] if i < 12 else ["S", "S", "V", "V"]) if i < 16 else ["S", "S", "S", "V"]
+        L = LAG
+        units = [(b, r) for b in range(B) for r in range(4)]
+
+        def m1u(i, g):
+            if i < 16:
+                if g == 0:
+                    h_tiles(units[i][0], units[i][1])
+                m1(units[i][0], units[i][1], g)
+
+        def hxu(i, e0, e1):
+            if i < 16:
+                hx(units[i][0], units[i][1], 0, e0)
+                hx(units[i][0], units[i][1], 1, e1)
+
+        def hqu(i):
+            if 0 <= i < 16:
+                hq(units[i][0], units[i][1])
+
+        def m2u(i):
+            if 0 <= i < 16:
+                m2(units[i][0], units[i][1], 0)
+                m2(units[i][0], units[i][1], 1)
+
+        def oxu(i, e0, e1):
+            if 0 <= i < 16:
+                o_tile(units[i][0], units[i][1])
+                ox(units[i][0], units[i][1], 0, e0)
+                ox(units[i][0], units[i][1], 1, e1)
+                st(units[i][0], units[i][1])
+
+        ld_x(0, 0, N)
+        ld_x(0, N, N + C)
+        ld_x(1, 0, N)
+        ld_w(0)
+        ld_w(1)
+        ld_x(1, N, N + C)
+        ld_x(2, 0, N)
+        ld_x(3, 0, N)
+        ld_x(2, N, N + C)
+        ld_x(3, N, N + C)
         make_identity(nc, ident_bf[:])
         make_identity(nc, ident_f[:])
         nc.vector.memset(warm[:], 1.0)
         nc.scalar.activation(out=warm[:], in_=warm[:], func=ACT.Sqrt)
-        ld_x(0, 0, N)
-        ld_x(0, N, N + C)
+
         deg_tiles(0)
         deg(0, 0, "S")
         deg(0, 1, "V")
-        ld_w(0)
         ch1(0)
         ch2(0)
         ch3(0)
         db(0)
-        f_tiles(0)
-        fr(0, 0, 256, "S")
-        fr(0, 256, 512, "V")
-        ld_w(1)
         tm(0, 0)
-        fr(0, 512, 768, "V")
+        f_tiles(0)
+        fr(0, 0, 256, "V")
+        fr(0, 256, 512, "V")
+        fr(0, 512, 768, "S")
         dbc(0)
-        fr(0, 768, 1024, "V")
-        tm(0, 1)
+        fr(0, 768, 1024, "S")
         f_tile(0)
-        f_v(0, 0)
-        f_v(0, 1)
-        wr(0, 0, 512, "S")
-        f_v(0, 2)
-        ld_x(1, 0, N + C)
-        f_v(0, 3)
+        for t in range(4):
+            f_v(0, t)
         fq(0, 0, 512)
         a_tiles(0)
-        ax(0, 0)
-        fq(0, 512, 1024)
+        tm(0, 1)
         tm(0, 2)
-        wr(0, 512, 1024, "S")
-        aq(0, 0, 1)
-        wr(1, 0, 512, "V")
-        h_tiles(0, 0)
-        m1(0, 0, 0)
-        m1(0, 0, 1)
-        ld_x(2, 0, N + C)
-        wr(1, 512, 1024, "V")
-        hx(0, 0, 0, "S")
-        hx(0, 0, 1, "S")
-        ax(0, 1)
-        wq(0, 0, 512)
-        tm(0, 3)
         deg_tiles(1)
         deg(1, 0, "S")
-        wq(1, 0, 512)
-        aq(0, 1, 1)
-        hq(0, 0)
         deg(1, 1, "S")
-        h_tiles(0, 1)
-        m1(0, 1, 0)
-        ld_x(3, 0, N + C)
-        wq(0, 512, 1024)
-        m2(0, 0, 0)
-        wq(1, 512, 1024)
-        m1(0, 1, 1)
-        ax(0, 2)
-        hx(0, 1, 0, "S")
-        m2(0, 0, 1)
+        ax(0, 0)
+        tm(0, 3)
+        fq(0, 512, 1024)
+        aq(0, 0, 1)
+        m1u(0, 0)
+        m1u(0, 1)
+        ax(0, 1)
         ch1(1)
-        hx(0, 1, 1, "S")
-        aq(0, 2, 1)
-        o_tile(0, 0)
-        ox(0, 0, 0, "V")
-        h_tiles(0, 2)
-        m1(0, 2, 0)
+        ax(0, 2)
+        aq(0, 1, 1)
         ch2(1)
-        ox(0, 0, 1, "S")
-        m1(0, 2, 1)
-        hq(0, 1)
         ch3(1)
-        ax(0, 3)
-        hx(0, 2, 0, "S")
+        aq(0, 2, 1)
         db(1)
-        st(0, 0)
-        f_tiles(1)
-        fr(1, 0, 256, "V")
-        hx(0, 2, 1, "S")
-        m2(0, 1, 0)
-        deg_tiles(2)
-        deg(2, 0, "S")
-        aq(0, 3, 1)
-        hq(0, 2)
-        fr(1, 256, 512, "V")
-        m2(0, 1, 1)
-        tm(1, 0)
-        fr(1, 512, 768, "V")
-        dbc(1)
-        h_tiles(0, 3)
-        m1(0, 3, 0)
-        m1(0, 3, 1)
-        fr(1, 768, 1024, "V")
-        o_tile(0, 1)
-        ox(0, 1, 0, "S")
-        tm(1, 1)
-        f_tile(1)
-        f_v(1, 0)
-        ox(0, 1, 1, "S")
-        m2(0, 2, 0)
-        f_v(1, 1)
-        f_v(1, 2)
-        hx(0, 3, 0, "S")
-        m2(0, 2, 1)
-        st(0, 1)
-        f_v(1, 3)
-        hx(0, 3, 1, "S")
-        fq(1, 0, 512)
-        o_tile(0, 2)
-        ox(0, 2, 0, "S")
-        a_tiles(1)
-        ax(1, 0)
-        ox(0, 2, 1, "S")
-        ax(1, 1)
-        tm(1, 2)
-        deg(2, 1, "S")
-        st(0, 2)
-        fq(1, 512, 1024)
-        tm(1, 3)
-        aq(1, 0, 2)
-        hq(0, 3)
-        h_tiles(1, 0)
-        m1(1, 0, 0)
-        ax(1, 2)
-        deg_tiles(3)
-        deg(3, 0, "S")
-        m2(0, 3, 0)
-        hx(1, 0, 0, "V")
-        m1(1, 0, 1)
-        m2(0, 3, 1)
-        ax(1, 3)
-        hx(1, 0, 1, "S")
-        h_tiles(1, 1)
-        m1(1, 1, 0)
-        ch1(2)
-        aq(1, 2, 2)
-        o_tile(0, 3)
-        ox(0, 3, 0, "S")
-        m1(1, 1, 1)
-        hq(1, 0)
-        h_tiles(1, 2)
-        m1(1, 2, 0)
-        f_tiles(2)
-        fr(2, 0, 256, "V")
-        ox(0, 3, 1, "S")
-        m2(1, 0, 0)
-        fr(2, 256, 512, "V")
-        hx(1, 1, 0, "S")
-        st(0, 3)
-        m2(1, 0, 1)
-        hx(1, 1, 1, "S")
-        o_tile(1, 0)
-        ox(1, 0, 0, "V")
-        m1(1, 2, 1)
-        h_tiles(1, 3)
-        m1(1, 3, 0)
-        ch2(2)
-        fr(2, 512, 768, "V")
-        ox(1, 0, 1, "S")
-        m1(1, 3, 1)
-        hx(1, 2, 0, "S")
-        hq(1, 1)
-        st(1, 0)
-        ch3(2)
-        fr(2, 768, 1024, "V")
-        db(2)
-        hx(1, 2, 1, "S")
-        fq(2, 0, 512)
-        hx(1, 3, 0, "S")
-        m2(1, 1, 0)
-        hq(1, 2)
-        hx(1, 3, 1, "S")
-        fq(2, 512, 1024)
-        m2(1, 1, 1)
-        dbc(2)
-        o_tile(1, 1)
-        ox(1, 1, 0, "V")
-        tm(2, 0)
-        ox(1, 1, 1, "S")
-        tm(2, 1)
-        f_tile(2)
-        f_v(2, 0)
-        m2(1, 2, 0)
-        f_v(2, 1)
-        deg(3, 1, "S")
-        st(1, 1)
-        f_v(2, 2)
-        m2(1, 2, 1)
-        f_v(2, 3)
-        hq(1, 3)
-        a_tiles(2)
-        ax(2, 0)
-        o_tile(1, 2)
-        ox(1, 2, 0, "S")
-        ax(2, 1)
-        ox(1, 2, 1, "S")
-        tm(2, 2)
-        m2(1, 3, 0)
-        ch1(3)
-        aq(2, 0, 2)
-        st(1, 2)
-        ch2(3)
-        ax(2, 2)
-        m2(1, 3, 1)
-        o_tile(1, 3)
-        ox(1, 3, 0, "S")
-        h_tiles(2, 0)
-        m1(2, 0, 0)
-        ch3(3)
-        f_tiles(3)
-        fr(3, 0, 256, "V")
-        ox(1, 3, 1, "S")
-        m1(2, 0, 1)
-        tm(2, 3)
-        fr(3, 256, 512, "V")
-        hx(2, 0, 0, "S")
-        st(1, 3)
-        h_tiles(2, 1)
-        m1(2, 1, 0)
-        m1(2, 1, 1)
-        hx(2, 0, 1, "S")
-        ax(2, 3)
-        db(3)
-        hx(2, 1, 0, "S")
-        hq(2, 0)
-        aq(2, 2, 2)
-        hx(2, 1, 1, "S")
-        m2(2, 0, 0)
-        fr(3, 512, 768, "V")
-        dbc(3)
-        m2(2, 0, 1)
-        hq(2, 1)
-        fr(3, 768, 1024, "V")
-        o_tile(2, 0)
-        ox(2, 0, 0, "S")
-        h_tiles(2, 2)
-        m1(2, 2, 0)
-        m1(2, 2, 1)
-        f_tile(3)
-        f_v(3, 0)
-        ox(2, 0, 1, "S")
-        tm(3, 0)
-        f_v(3, 1)
-        m2(2, 1, 0)
-        f_v(3, 2)
-        hx(2, 2, 0, "S")
-        st(2, 0)
-        f_v(3, 3)
-        m2(2, 1, 1)
-        hx(2, 2, 1, "S")
-        o_tile(2, 1)
-        ox(2, 1, 0, "V")
-        tm(3, 1)
-        ox(2, 1, 1, "S")
-        hq(2, 2)
-        h_tiles(2, 3)
-        m1(2, 3, 0)
-        a_tiles(3)
-        ax(3, 0)
-        m1(2, 3, 1)
-        hx(2, 3, 0, "S")
-        st(2, 1)
-        m2(2, 2, 0)
-        ax(3, 1)
-        hx(2, 3, 1, "S")
-        m2(2, 2, 1)
-        fq(3, 0, 512)
-        o_tile(2, 2)
-        ox(2, 2, 0, "S")
-        tm(3, 2)
-        aq(3, 0, 2)
-        tm(3, 3)
-        ox(2, 2, 1, "S")
-        fq(3, 512, 1024)
-        h_tiles(3, 0)
-        m1(3, 0, 0)
-        hq(2, 3)
-        st(2, 2)
-        hx(3, 0, 0, "S")
-        m1(3, 0, 1)
-        ax(3, 2)
-        m2(2, 3, 0)
-        hx(3, 0, 1, "S")
-        ax(3, 3)
-        m2(2, 3, 1)
-        o_tile(2, 3)
-        ox(2, 3, 0, "S")
-        hq(3, 0)
-        h_tiles(3, 1)
-        m1(3, 1, 0)
-        aq(3, 2, 2)
-        ox(2, 3, 1, "S")
-        m1(3, 1, 1)
-        m2(3, 0, 0)
-        hx(3, 1, 1, "V")
-        hx(3, 1, 0, "S")
-        st(2, 3)
-        m2(3, 0, 1)
-        o_tile(3, 0)
-        ox(3, 0, 0, "S")
-        hq(3, 1)
-        h_tiles(3, 2)
-        m1(3, 2, 0)
-        m1(3, 2, 1)
-        ox(3, 0, 1, "S")
-        hx(3, 2, 0, "V")
-        m2(3, 1, 0)
-        hx(3, 2, 1, "S")
-        st(3, 0)
-        m2(3, 1, 1)
-        o_tile(3, 1)
-        ox(3, 1, 0, "S")
-        hq(3, 2)
-        h_tiles(3, 3)
-        m1(3, 3, 0)
-        m1(3, 3, 1)
-        ox(3, 1, 1, "S")
-        hx(3, 3, 0, "V")
-        m2(3, 2, 0)
-        hx(3, 3, 1, "S")
-        st(3, 1)
-        m2(3, 2, 1)
-        o_tile(3, 2)
-        ox(3, 2, 0, "S")
-        hq(3, 3)
-        ox(3, 2, 1, "S")
-        m2(3, 3, 0)
-        m2(3, 3, 1)
-        st(3, 2)
-        o_tile(3, 3)
-        ox(3, 3, 0, "S")
-        ox(3, 3, 1, "S")
-        st(3, 3)
+
+        for i in range(16 + L + 2):
+            ex = EX(i)
+            b = i // 4
+            r = i % 4
+            if 4 <= i + 4 < 16:
+                tm(units[i + 4][0], units[i + 4][1])
+            if i + 3 < 16:
+                if r == 1:
+                    a_tiles(b + 1)
+                ax(units[i + 3][0], units[i + 3][1])
+            hqu(i - 1)
+            if 1 <= i <= 2:
+                wq(i - 1, 0, O)
+            if r == 2 and b + 2 < B:
+                ch1(b + 2)
+            if r == 3 and b + 2 < B:
+                ch3(b + 2)
+            if i < 2:
+                wr(i, 512, 1024, "V")
+            if b + 1 < B:
+                if r == 0:
+                    f_tiles(b + 1)
+                fr(b + 1, 256 * r, 256 * r + 256, "V")
+            oxu(i - L - 1, ex[2], ex[3])
+            hxu(i, ex[0], ex[1])
+            if r == 0 and b + 1 < B:
+                dbc(b + 1)
+            if i + 3 < 16:
+                aq(units[i + 3][0], units[i + 3][1], 1)
+            if b + 1 < B:
+                fq(b + 1, 256 * r, 256 * r + 256)
+            if i < 2:
+                wr(i, 0, 512, "S")
+            m1u(i + 1, 0)
+            m2u(i - L)
+            m1u(i + 1, 1)
+            if r == 3 and b + 2 < B:
+                db(b + 2)
+            if r == 0 and b + 1 < B:
+                f_tile(b + 1)
+                for t in range(4):
+                    f_v(b + 1, t)
+            if r < 2 and b + 2 < B:
+                if r == 0:
+                    deg_tiles(b + 2)
+                deg(b + 2, r, "S")
+            if r == 2 and b + 2 < B:
+                ch2(b + 2)

@@ -3,7 +3,8 @@ from contextlib import ExitStack
 import concourse.mybir as mybir
 from concourse.masks import make_identity
 
-FLOPS = 2 * 4 * 512 * 512 * 1024 + 2 * 4 * 512 * 1024 * 1024
+B, N, C, O = 4, 512, 1024, 1024
+FLOPS = 2 * B * N * N * C + 2 * B * N * C * O
 
 FP8X4 = mybir.dt.float8_e4m3fn_x4
 BF16 = mybir.dt.bfloat16
@@ -12,325 +13,267 @@ U32 = mybir.dt.uint32
 U8 = mybir.dt.uint8
 ALU = mybir.AluOpType
 ACT = mybir.ActivationFunctionType
-AXIS = mybir.AxisListType
 
 P = 128
-B, N, C, O = 4, 512, 1024, 1024
-HB = 8
-PTB = 3
-PHB = 3
+PACK = 4
+TILES = N // P
+UNITS = B * TILES
+HALF = 512
+QUARTER = C // 4
 
 
 def tile_gcnconv_pa_kernel(tc, X, W, out):
     nc = tc.nc
     with ExitStack() as ctx:
         keep = ctx.enter_context(tc.tile_pool(name="keep", bufs=1))
-        rot = ctx.enter_context(tc.tile_pool(name="rot", bufs=2))
-        psum = ctx.enter_context(tc.psum_pool(name="psum", bufs=2))
-        ctx.enter_context(tc.manual_schedule())
+        graph = ctx.enter_context(tc.tile_pool(name="graph", bufs=B))
+        stage = ctx.enter_context(tc.tile_pool(name="stage", bufs=2))
+        psum = ctx.enter_context(tc.psum_pool(name="psum", bufs=8))
 
         ident_bf = keep.tile([P, P], BF16, name="ident_bf")
         ident_f = keep.tile([P, P], F32, name="ident_f")
-        warm = keep.tile([P, 1], F32, name="warm")
-        junk = keep.tile([P, N], BF16, name="junk")
-        xs = [keep.tile([P, 4, N + C], BF16, name="xs%d" % b) for b in range(B)]
-        ws = keep.tile([P, 8, O], BF16, name="ws")
-        wg = keep.tile([P, 2, O, 4], BF16, name="wg", align_bytes=64)
-        wc = keep.tile([P, 2, O], U32, name="wc", align_bytes=64)
-        wsc = keep.tile([P, 2, O], U8, name="wsc", align_bytes=64)
-        T = {}
+        one = keep.tile([P, 1], F32, name="one")
+        unused = keep.tile([P, N], BF16, name="unused")
+        x_sb = [keep.tile([P, PACK, N + C], BF16, name="x_sb%d" % b) for b in range(B)]
+        w_sb = keep.tile([P, 2 * PACK, O], BF16, name="w_sb")
+        w_grp = keep.tile([P, 2, O, PACK], BF16, name="w_grp", align_bytes=64)
+        w_code = keep.tile([P, 2, O], U32, name="w_code", align_bytes=64)
+        w_scale = keep.tile([P, 2, O], U8, name="w_scale", align_bytes=64)
+        tiles = {}
 
-        Xv = X.rearrange("b (t p) w -> b p t w", p=P)
-        Wv = W.rearrange("(g p) o -> p g o", p=P)
+        x_view = X.rearrange("b (t p) w -> b p t w", p=P)
+        w_view = W.rearrange("(j p) o -> p j o", p=P)
 
-        def ld_x(b, lo, hi):
-            nc.sync.dma_start(out=xs[b][:, :, lo:hi], in_=Xv[b][:, :, lo:hi])
+        def load_x(b, lo, hi, first=0, last=PACK):
+            nc.sync.dma_start(out=x_sb[b][:, first:last, lo:hi], in_=x_view[b][:, first:last, lo:hi])
 
-        def ld_w(g):
-            nc.sync.dma_start(out=ws[:, 4 * g:4 * g + 4, :], in_=Wv[:, 4 * g:4 * g + 4, :])
+        def load_w(s):
+            rows = slice(PACK * s, PACK * s + PACK)
+            nc.sync.dma_start(out=w_sb[:, rows, :], in_=w_view[:, rows, :])
 
-        def copy_on(eng, dst, src):
-            if eng == "V":
+        def copy_on(engine, dst, src):
+            if engine == "vector":
                 nc.vector.tensor_copy(out=dst, in_=src)
             else:
                 nc.scalar.copy(out=dst, in_=src)
 
-        def regroup(eng, dst, src):
-            copy_on(eng, dst.rearrange("p (c i) t -> p c t i", i=4), src.rearrange("p t (c i) -> p c t i", i=4))
+        def group(engine, dst, src):
+            copy_on(engine, dst.rearrange("p (c i) t -> p c t i", i=4), src.rearrange("p t (c i) -> p c t i", i=4))
 
-        def deg_tiles(b):
-            T["deg", b] = rot.tile([P, 2, 8], F32, name="deg", bufs=4)
+        def quantise(code, scale, grouped):
+            nc.vector.quantize_mx(out=code.bitcast(FP8X4), scales=scale, in_=grouped)
 
-        def deg_s(b, t):
-            nc.scalar.activation(out=junk[:], in_=xs[b][:, t, 0:N], func=ACT.Copy,
-                                 accum_out=T["deg", b][:, t // 2, t % 2:t % 2 + 1])
+        def degrees(b, first, last):
+            if first == 0:
+                tiles["deg", b] = graph.tile([P, PACK], F32, name="deg")
+            for t in range(first, last):
+                nc.scalar.activation(out=unused[:], in_=x_sb[b][:, t, 0:N], func=ACT.Copy, accum_out=tiles["deg", b][:, t:t + 1])
 
-        def deg_v(b, h):
-            nc.vector.tensor_reduce(out=T["deg", b][:, h, 0:2], in_=xs[b][:, 2 * h:2 * h + 2, 0:N], axis=AXIS.X, op=ALU.add)
+        def root_degrees(b):
+            root = graph.tile([P, PACK], F32, name="root")
+            tiles["root", b] = root
+            nc.scalar.activation(out=root[:], in_=tiles["deg", b][:], func=ACT.Sqrt)
 
-        def deg(b, h, eng):
-            if eng == "V":
-                deg_v(b, h)
-            else:
-                deg_s(b, 2 * h)
-                deg_s(b, 2 * h + 1)
+        def invert_roots(b):
+            deg = tiles["deg", b]
+            safe = graph.tile([P, PACK], F32, name="safe")
+            recip = graph.tile([P, PACK], F32, name="recip")
+            dinv = graph.tile([P, PACK], F32, name="dinv")
+            tiles["dinv", b] = dinv
+            nc.vector.scalar_tensor_tensor(out=safe[:], in0=deg[:], scalar=0.0, in1=tiles["root", b][:], op0=ALU.is_le, op1=ALU.max)
+            nc.vector.reciprocal(out=recip[:], in_=safe[:])
+            nc.vector.scalar_tensor_tensor(out=dinv[:], in0=deg[:], scalar=0.0, in1=recip[:], op0=ALU.is_gt, op1=ALU.mult)
 
-        def ch1(b):
-            safe = rot.tile([P, 2, 2], F32, name="safe", bufs=4)
-            T["safe", b] = safe
-            dg = T["deg", b][:, :, 0:2]
-            nc.vector.scalar_tensor_tensor(out=safe[:], in0=dg, scalar=0.0, in1=dg, op0=ALU.is_le, op1=ALU.max)
-
-        def ch2(b):
-            sq = rot.tile([P, 2, 2], F32, name="sq", bufs=4)
-            T["sq", b] = sq
-            nc.scalar.activation(out=sq[:], in_=T["safe", b][:], func=ACT.Sqrt)
-
-        def ch3(b):
-            rc = rot.tile([P, 2, 2], F32, name="rc", bufs=4)
-            d = rot.tile([P, 4], F32, name="d", bufs=4)
-            T["d", b] = d
-            nc.vector.reciprocal(out=rc[:], in_=T["sq", b][:])
-            nc.vector.scalar_tensor_tensor(out=d[:].rearrange("p (h c) -> p h c", c=2), in0=T["deg", b][:, :, 0:2], scalar=0.0,
-                                           in1=rc[:], op0=ALU.is_gt, op1=ALU.mult)
-
-        def db(b):
-            pdb = psum.tile([P, N], F32, name="bank", bufs=8)
-            T["pdb", b] = pdb
-            for t in range(4):
-                nc.tensor.matmul(out=pdb[:, t * P:(t + 1) * P], lhsT=T["d", b][:, t:t + 1].to_broadcast([P, P]), rhs=ident_f[:],
+        def spread_dinv(b):
+            bank = psum.tile([P, N], F32, name="bank")
+            tiles["dinv_bank", b] = bank
+            for t in range(PACK):
+                nc.tensor.matmul(out=bank[:, t * P:(t + 1) * P], lhsT=tiles["dinv", b][:, t:t + 1].to_broadcast([P, P]), rhs=ident_f[:],
                                  start=True, stop=True)
 
-        def dbc(b):
-            t_ = rot.tile([P, N], F32, name="dbc", bufs=4)
-            T["dbc", b] = t_
-            nc.scalar.copy(out=t_[:], in_=T["pdb", b][:])
+        def fetch_dinv_row(b):
+            row = graph.tile([P, N], F32, name="dinv_row")
+            tiles["dinv_row", b] = row
+            nc.scalar.copy(out=row[:], in_=tiles["dinv_bank", b][:])
 
-        def f_tile(b):
-            T["F", b] = rot.tile([P, 4, N], F32, name="F")
+        def pair_factors(b):
+            pair = stage.tile([P, PACK, N], F32, name="pair")
+            tiles["pair", b] = pair
+            for t in range(PACK):
+                nc.vector.tensor_scalar(out=pair[:, t, :], in0=tiles["dinv_row", b][:], scalar1=tiles["dinv", b][:, t:t + 1], scalar2=None, op0=ALU.mult)
 
-        def f_v(b, t):
-            nc.vector.tensor_scalar(out=T["F", b][:, t, :], in0=T["dbc", b][:], scalar1=T["d", b][:, t:t + 1], scalar2=None, op0=ALU.mult)
-
-        def f_s(b, t):
-            nc.scalar.activation(out=T["F", b][:, t, :], in_=T["pdb", b][:], func=ACT.Copy, scale=T["d", b][:, t:t + 1])
-
-        def tm(b, r):
-            pat = psum.tile([P, 4, P], F32, name="bank", bufs=8)
-            T["pat", b, r] = pat
-            for t in range(4):
-                nc.tensor.matmul(out=pat[:, t, :], lhsT=xs[b][:, r, t * P:(t + 1) * P], rhs=ident_bf[:], start=True, stop=(t != r))
+        def transpose_adjacency(b, r):
+            bank = psum.tile([P, PACK, P], F32, name="bank")
+            tiles["a_bank", b, r] = bank
+            for t in range(PACK):
+                nc.tensor.matmul(out=bank[:, t, :], lhsT=x_sb[b][:, r, t * P:(t + 1) * P], rhs=ident_bf[:], start=True, stop=(t != r))
                 if t == r:
-                    nc.tensor.matmul(out=pat[:, t, :], lhsT=ident_bf[:], rhs=ident_bf[:], start=False, stop=True)
+                    nc.tensor.matmul(out=bank[:, t, :], lhsT=ident_bf[:], rhs=ident_bf[:], start=False, stop=True)
 
-        def a_tiles(b):
-            T["ag", b] = rot.tile([P, 4, P, 4], BF16, name="ag", bufs=4, align_bytes=64)
-            T["ac", b] = rot.tile([P, N], U32, name="ac", bufs=4, align_bytes=64)
-            T["as", b] = rot.tile([P, N], U8, name="as", bufs=4, align_bytes=64)
+        def scale_adjacency(b, r):
+            if ("a_grp", b) not in tiles:
+                tiles["a_grp", b] = graph.tile([P, TILES, P, PACK], BF16, name="a_grp", align_bytes=64)
+                tiles["a_code", b] = graph.tile([P, N], U32, name="a_code", align_bytes=64)
+                tiles["a_scale", b] = graph.tile([P, N], U8, name="a_scale", align_bytes=64)
+            nc.vector.tensor_tensor(out=tiles["a_grp", b][:, r, :, :], in0=tiles["a_bank", b, r][:].rearrange("p t j -> p j t"),
+                                    in1=tiles["pair", b][:, :, r * P:(r + 1) * P].rearrange("p t j -> p j t"), op=ALU.mult)
 
-        def ax(b, r):
-            nc.vector.tensor_tensor(out=T["ag", b][:, r, :, :], in0=T["pat", b, r][:].rearrange("p t n -> p n t"),
-                                    in1=T["F", b][:, :, r * P:(r + 1) * P].rearrange("p t n -> p n t"), op=ALU.mult)
+        def quantise_adjacency(b, r):
+            cols = slice(r * P, (r + 1) * P)
+            quantise(tiles["a_code", b][:, cols], tiles["a_scale", b][:, cols], tiles["a_grp", b][:, r, :, :].rearrange("p j t -> p (j t)"))
 
-        def aq(b, r0, nr):
-            cols = slice(r0 * P, (r0 + nr) * P)
-            nc.vector.quantize_mx(out=T["ac", b][:, cols].bitcast(FP8X4), scales=T["as", b][:, cols],
-                                  in_=T["ag", b][:, r0:r0 + nr, :, :].rearrange("p r n t -> p (r n t)"))
+        def group_features(b, lo, hi, engine):
+            if ("f_grp", b) not in tiles:
+                tiles["f_grp", b] = stage.tile([P, C, PACK], BF16, name="f_grp", align_bytes=64)
+                tiles["f_code", b] = graph.tile([P, C], U32, name="f_code", align_bytes=64)
+                tiles["f_scale", b] = graph.tile([P, C], U8, name="f_scale", align_bytes=64)
+            group(engine, tiles["f_grp", b][:, lo:hi, :], x_sb[b][:, :, N + lo:N + hi])
 
-        def f_tiles(b):
-            T["fg", b] = rot.tile([P, C, 4], BF16, name="fg", align_bytes=64)
-            T["fc", b] = rot.tile([P, C], U32, name="fc", bufs=4, align_bytes=64)
-            T["fs", b] = rot.tile([P, C], U8, name="fs", bufs=4, align_bytes=64)
+        def quantise_features(b, lo, hi):
+            quantise(tiles["f_code", b][:, lo:hi], tiles["f_scale", b][:, lo:hi], tiles["f_grp", b][:, lo:hi, :].rearrange("p c t -> p (c t)"))
 
-        def fr(b, c0, c1, eng):
-            regroup(eng, T["fg", b][:, c0:c1, :], xs[b][:, :, N + c0:N + c1])
+        def group_weights(s, lo, hi, engine):
+            group(engine, w_grp[:, s, lo:hi, :], w_sb[:, PACK * s:PACK * s + PACK, lo:hi])
 
-        def fq(b, c0, c1):
-            nc.vector.quantize_mx(out=T["fc", b][:, c0:c1].bitcast(FP8X4), scales=T["fs", b][:, c0:c1],
-                                  in_=T["fg", b][:, c0:c1, :].rearrange("p c t -> p (c t)"))
+        def quantise_weights(s):
+            quantise(w_code[:, s, :], w_scale[:, s, :], w_grp[:, s, :, :].rearrange("p o t -> p (o t)"))
 
-        def wr(g, o0, o1, eng):
-            regroup(eng, wg[:, g, o0:o1, :], ws[:, 4 * g:4 * g + 4, o0:o1])
+        def first_product(u, s):
+            b, r = divmod(u, TILES)
+            bank = psum.tile([P, PACK, P], F32, name="bank")
+            tiles["h_bank", u, s] = bank
+            nodes = slice(r * P, (r + 1) * P)
+            for t in range(PACK):
+                feats = slice((PACK * s + t) * P, (PACK * s + t + 1) * P)
+                nc.tensor.matmul_mx(out=bank[:, t, :], lhsT=tiles["f_code", b][:, feats].bitcast(FP8X4), lhsT_scale=tiles["f_scale", b][:, feats],
+                                    rhs=tiles["a_code", b][:, nodes].bitcast(FP8X4), rhs_scale=tiles["a_scale", b][:, nodes], start=True, stop=True)
 
-        def wq(g, o0, o1):
-            nc.vector.quantize_mx(out=wc[:, g, o0:o1].bitcast(FP8X4), scales=wsc[:, g, o0:o1],
-                                  in_=wg[:, g, o0:o1, :].rearrange("p o t -> p (o t)"))
+        def fetch_hidden(u, s, engine):
+            if s == 0:
+                tiles["h_grp", u] = stage.tile([P, 2, P, PACK], BF16, name="h_grp", bufs=4, align_bytes=64)
+            copy_on(engine, tiles["h_grp", u][:, s, :, :], tiles["h_bank", u, s][:].rearrange("p t j -> p j t"))
 
-        def h_tiles(b, r):
-            T["hg", b, r] = rot.tile([P, 2, P, 4], BF16, name="hg", bufs=HB, align_bytes=64)
-            T["hc", b, r] = rot.tile([P, 2 * P], U32, name="hc", bufs=HB, align_bytes=64)
-            T["hs", b, r] = rot.tile([P, 2 * P], U8, name="hs", bufs=HB, align_bytes=64)
+        def quantise_hidden(u):
+            tiles["h_code", u] = stage.tile([P, 2 * P], U32, name="h_code", bufs=4, align_bytes=64)
+            tiles["h_scale", u] = stage.tile([P, 2 * P], U8, name="h_scale", bufs=4, align_bytes=64)
+            quantise(tiles["h_code", u][:], tiles["h_scale", u][:], tiles["h_grp", u][:].rearrange("p s j t -> p (s j t)"))
 
-        def o_tile(b, r):
-            T["ost", b, r] = rot.tile([P, O], F32, name="ost", bufs=4)
+        def second_product(u, half):
+            bank = psum.tile([P, HALF], F32, name="bank")
+            tiles["o_bank", u, half] = bank
+            cols = slice(half * HALF, (half + 1) * HALF)
+            for s in range(2):
+                nodes = slice(s * P, (s + 1) * P)
+                nc.tensor.matmul_mx(out=bank[:], lhsT=tiles["h_code", u][:, nodes].bitcast(FP8X4), lhsT_scale=tiles["h_scale", u][:, nodes],
+                                    rhs=w_code[:, s, cols].bitcast(FP8X4), rhs_scale=w_scale[:, s, cols], start=(s == 0), stop=(s == 1))
 
-        def m1(b, r, g):
-            ph = psum.tile([P, 4, P], F32, name="bank", bufs=8)
-            T["ph", b, r, g] = ph
-            ncol = slice(r * P, (r + 1) * P)
-            for t in range(4):
-                ccol = slice((4 * g + t) * P, (4 * g + t + 1) * P)
-                nc.tensor.matmul_mx(out=ph[:, t, :], lhsT=T["fc", b][:, ccol].bitcast(FP8X4), lhsT_scale=T["fs", b][:, ccol],
-                                    rhs=T["ac", b][:, ncol].bitcast(FP8X4), rhs_scale=T["as", b][:, ncol], start=True, stop=True)
-
-        def hx(b, r, g, eng):
-            copy_on(eng, T["hg", b, r][:, g, :, :], T["ph", b, r, g][:].rearrange("p t n -> p n t"))
-
-        def hq(b, r):
-            nc.vector.quantize_mx(out=T["hc", b, r][:].bitcast(FP8X4), scales=T["hs", b, r][:],
-                                  in_=T["hg", b, r][:].rearrange("p g n t -> p (g n t)"))
-
-        def m2(b, r, oh):
-            po = psum.tile([P, 512], F32, name="bank", bufs=8)
-            T["po", b, r, oh] = po
-            ocol = slice(oh * 512, (oh + 1) * 512)
-            for g in range(2):
-                ncol = slice(g * P, (g + 1) * P)
-                nc.tensor.matmul_mx(out=po[:], lhsT=T["hc", b, r][:, ncol].bitcast(FP8X4), lhsT_scale=T["hs", b, r][:, ncol],
-                                    rhs=wc[:, g, ocol].bitcast(FP8X4), rhs_scale=wsc[:, g, ocol], start=(g == 0), stop=(g == 1))
-
-        def ox(b, r, oh, eng):
-            dst = T["ost", b, r][:, oh * 512:(oh + 1) * 512]
-            if eng == "V":
-                nc.vector.tensor_scalar_max(out=dst, in0=T["po", b, r, oh][:], scalar1=0.0)
+        def store_output(u, half, engine):
+            b, r = divmod(u, TILES)
+            o_sb = stage.tile([P, HALF], F32, name="o_sb", bufs=8)
+            if engine == "vector":
+                nc.vector.tensor_scalar_max(out=o_sb[:], in0=tiles["o_bank", u, half][:], scalar1=0.0)
             else:
-                nc.scalar.activation(out=dst, in_=T["po", b, r, oh][:], func=ACT.Relu)
+                nc.scalar.activation(out=o_sb[:], in_=tiles["o_bank", u, half][:], func=ACT.Relu)
+            nc.sync.dma_start(out=out[b, r * P:(r + 1) * P, half * HALF:(half + 1) * HALF], in_=o_sb[:])
 
-        def st(b, r):
-            nc.sync.dma_start(out=out[b, r * P:(r + 1) * P, :], in_=T["ost", b, r][:])
-
-        LAG = 2
-        def EX(i):
-            return (["S", "S", "S", "V" if (i % 4 < 2) else "S"] if i < 12 else ["S", "S", "V", "V"]) if i < 16 else ["S", "S", "S", "V"]
-        L = LAG
-        units = [(b, r) for b in range(B) for r in range(4)]
-
-        def m1u(i, g):
-            if i < 16:
-                if g == 0:
-                    h_tiles(units[i][0], units[i][1])
-                m1(units[i][0], units[i][1], g)
-
-        def hxu(i, e0, e1):
-            if i < 16:
-                hx(units[i][0], units[i][1], 0, e0)
-                hx(units[i][0], units[i][1], 1, e1)
-
-        def hqu(i):
-            if 0 <= i < 16:
-                hq(units[i][0], units[i][1])
-
-        def m2u(i):
-            if 0 <= i < 16:
-                m2(units[i][0], units[i][1], 0)
-                m2(units[i][0], units[i][1], 1)
-
-        def oxu(i, e0, e1):
-            if 0 <= i < 16:
-                o_tile(units[i][0], units[i][1])
-                ox(units[i][0], units[i][1], 0, e0)
-                ox(units[i][0], units[i][1], 1, e1)
-                st(units[i][0], units[i][1])
-
-        ld_x(0, 0, N)
-        ld_x(0, N, N + C)
-        ld_x(1, 0, N)
-        ld_w(0)
-        ld_w(1)
-        ld_x(1, N, N + C)
-        ld_x(2, 0, N)
-        ld_x(3, 0, N)
-        ld_x(2, N, N + C)
-        ld_x(3, N, N + C)
+        load_x(0, 0, N, 0, 2)
+        load_x(0, 0, N, 2, PACK)
+        load_x(0, N, N + C)
+        load_x(1, 0, N)
+        load_w(0)
+        load_w(1)
+        load_x(1, N, N + C)
+        load_x(2, 0, N)
+        load_x(3, 0, N)
+        load_x(2, N, N + C)
+        load_x(3, N, N + C)
         make_identity(nc, ident_bf[:])
         make_identity(nc, ident_f[:])
-        nc.vector.memset(warm[:], 1.0)
-        nc.scalar.activation(out=warm[:], in_=warm[:], func=ACT.Sqrt)
+        nc.vector.memset(one[:], 1.0)
+        nc.scalar.activation(out=one[:], in_=one[:], func=ACT.Sqrt)
 
-        deg_tiles(0)
-        deg(0, 0, "S")
-        deg(0, 1, "V")
-        ch1(0)
-        ch2(0)
-        ch3(0)
-        db(0)
-        tm(0, 0)
-        f_tiles(0)
-        fr(0, 0, 256, "V")
-        fr(0, 256, 512, "V")
-        fr(0, 512, 768, "S")
-        dbc(0)
-        fr(0, 768, 1024, "S")
-        f_tile(0)
-        for t in range(4):
-            f_v(0, t)
-        fq(0, 0, 512)
-        a_tiles(0)
-        tm(0, 1)
-        tm(0, 2)
-        deg_tiles(1)
-        deg(1, 0, "S")
-        deg(1, 1, "S")
-        ax(0, 0)
-        tm(0, 3)
-        fq(0, 512, 1024)
-        aq(0, 0, 1)
-        m1u(0, 0)
-        m1u(0, 1)
-        ax(0, 1)
-        ch1(1)
-        ax(0, 2)
-        aq(0, 1, 1)
-        ch2(1)
-        ch3(1)
-        aq(0, 2, 1)
-        db(1)
+        degrees(0, 0, PACK)
+        root_degrees(0)
+        invert_roots(0)
+        spread_dinv(0)
+        transpose_adjacency(0, 0)
+        group_features(0, 0, QUARTER, "vector")
+        group_features(0, QUARTER, 2 * QUARTER, "vector")
+        group_features(0, 2 * QUARTER, 3 * QUARTER, "scalar")
+        fetch_dinv_row(0)
+        group_features(0, 3 * QUARTER, C, "scalar")
+        quantise_features(0, 0, 2 * QUARTER)
+        pair_factors(0)
+        transpose_adjacency(0, 1)
+        transpose_adjacency(0, 2)
+        degrees(1, 0, PACK)
+        scale_adjacency(0, 0)
+        transpose_adjacency(0, 3)
+        quantise_features(0, 2 * QUARTER, C)
+        quantise_adjacency(0, 0)
+        first_product(0, 0)
+        first_product(0, 1)
+        root_degrees(1)
+        scale_adjacency(0, 1)
+        scale_adjacency(0, 2)
+        quantise_adjacency(0, 1)
+        invert_roots(1)
+        quantise_adjacency(0, 2)
+        spread_dinv(1)
+        group_weights(0, 0, HALF, "scalar")
+        group_weights(0, HALF, O, "vector")
 
-        for i in range(16 + L + 2):
-            ex = EX(i)
-            b = i // 4
-            r = i % 4
-            if 4 <= i + 4 < 16:
-                tm(units[i + 4][0], units[i + 4][1])
-            if i + 3 < 16:
-                if r == 1:
-                    a_tiles(b + 1)
-                ax(units[i + 3][0], units[i + 3][1])
-            hqu(i - 1)
-            if 1 <= i <= 2:
-                wq(i - 1, 0, O)
-            if r == 2 and b + 2 < B:
-                ch1(b + 2)
-            if r == 3 and b + 2 < B:
-                ch3(b + 2)
+        for i in range(UNITS + 2):
+            b, r = divmod(i, TILES)
+            nxt = b + 1
+            far = b + 2
+            if nxt >= B and i < UNITS:
+                store_engines = ("vector", "vector")
+            elif r < 2 or i >= UNITS:
+                store_engines = ("scalar", "vector")
+            else:
+                store_engines = ("scalar", "scalar")
+
+            if TILES <= i + 4 < UNITS:
+                transpose_adjacency((i + 4) // TILES, (i + 4) % TILES)
+            if i + 3 < UNITS:
+                scale_adjacency((i + 3) // TILES, (i + 3) % TILES)
+            if 1 <= i <= UNITS:
+                quantise_hidden(i - 1)
             if i < 2:
-                wr(i, 512, 1024, "V")
-            if b + 1 < B:
-                if r == 0:
-                    f_tiles(b + 1)
-                fr(b + 1, 256 * r, 256 * r + 256, "V")
-            oxu(i - L - 1, ex[2], ex[3])
-            hxu(i, ex[0], ex[1])
-            if r == 0 and b + 1 < B:
-                dbc(b + 1)
-            if i + 3 < 16:
-                aq(units[i + 3][0], units[i + 3][1], 1)
-            if b + 1 < B:
-                fq(b + 1, 256 * r, 256 * r + 256)
-            if i < 2:
-                wr(i, 0, 512, "S")
-            m1u(i + 1, 0)
-            m2u(i - L)
-            m1u(i + 1, 1)
-            if r == 3 and b + 2 < B:
-                db(b + 2)
-            if r == 0 and b + 1 < B:
-                f_tile(b + 1)
-                for t in range(4):
-                    f_v(b + 1, t)
-            if r < 2 and b + 2 < B:
-                if r == 0:
-                    deg_tiles(b + 2)
-                deg(b + 2, r, "S")
-            if r == 2 and b + 2 < B:
-                ch2(b + 2)
+                quantise_weights(i)
+            if r == 3 and far < B:
+                invert_roots(far)
+            if i == 0:
+                group_weights(1, HALF, O, "vector")
+            if nxt < B:
+                group_features(nxt, r * QUARTER, (r + 1) * QUARTER, "vector")
+            if i >= 2:
+                store_output(i - 2, 0, store_engines[0])
+                store_output(i - 2, 1, store_engines[1])
+            if i < UNITS:
+                fetch_hidden(i, 0, "scalar")
+                fetch_hidden(i, 1, "scalar")
+            if r == 0 and nxt < B:
+                fetch_dinv_row(nxt)
+            if i + 3 < UNITS:
+                quantise_adjacency((i + 3) // TILES, (i + 3) % TILES)
+            if nxt < B:
+                quantise_features(nxt, r * QUARTER, (r + 1) * QUARTER)
+            if i == 0:
+                group_weights(1, 0, HALF, "scalar")
+            if i + 1 < UNITS:
+                first_product(i + 1, 0)
+            if 1 <= i <= UNITS:
+                second_product(i - 1, 0)
+                second_product(i - 1, 1)
+            if i + 1 < UNITS:
+                first_product(i + 1, 1)
+            if r == 3 and far < B:
+                spread_dinv(far)
+            if r == 0 and nxt < B:
+                pair_factors(nxt)
+            if r < 2 and far < B:
+                degrees(far, 2 * r, 2 * r + 2)
+            if r == 1 and far < B:
+                root_degrees(far)

@@ -229,7 +229,7 @@ def tile_gcnconv_pa_kernel(tc, X, W, out):
             far = b + 2
             if nxt >= B and i < UNITS:
                 store_engines = ("vector", "vector")
-            elif r < 2 or i >= UNITS:
+            elif r == 1 or i >= UNITS:
                 store_engines = ("scalar", "vector")
             else:
                 store_engines = ("scalar", "scalar")

@@ -85,11 +85,13 @@ def tile_gcnconv_pa_kernel(tc, X, W, out):
             nc.vector.scalar_tensor_tensor(out=dinv[:], in0=deg[:], scalar=0.0, in1=recip[:], op0=ALU.is_gt, op1=ALU.mult)
 
         def spread_dinv(b):
+            repeated = stage.tile([P, PACK, P], F32, name="repeated")
+            nc.gpsimd.tensor_scalar(out=repeated[:], in0=tiles["dinv", b][:].unsqueeze(2).to_broadcast([P, PACK, P]), scalar1=1.0, scalar2=0.0,
+                                    op0=ALU.mult, op1=ALU.add)
             bank = psum.tile([P, N], F32, name="bank")
             tiles["dinv_bank", b] = bank
             for t in range(PACK):
-                nc.tensor.matmul(out=bank[:, t * P:(t + 1) * P], lhsT=tiles["dinv", b][:, t:t + 1].to_broadcast([P, P]), rhs=ident_f[:],
-                                 start=True, stop=True)
+                nc.tensor.transpose(out=bank[:, t * P:(t + 1) * P], in_=repeated[:, t, :], identity=ident_f[:])
 
         def fetch_dinv_row(b):
             row = graph.tile([P, N], F32, name="dinv_row")
@@ -199,9 +201,9 @@ def tile_gcnconv_pa_kernel(tc, X, W, out):
         transpose_adjacency(0, 0)
         group_features(0, 0, QUARTER, "vector")
         group_features(0, QUARTER, 2 * QUARTER, "vector")
-        group_features(0, 2 * QUARTER, 3 * QUARTER, "scalar")
+        group_features(0, 2 * QUARTER, 3 * QUARTER, "vector")
         fetch_dinv_row(0)
-        group_features(0, 3 * QUARTER, C, "scalar")
+        group_features(0, 3 * QUARTER, C, "vector")
         quantise_features(0, 0, 2 * QUARTER)
         pair_factors(0)
         transpose_adjacency(0, 1)
@@ -220,16 +222,14 @@ def tile_gcnconv_pa_kernel(tc, X, W, out):
         invert_roots(1)
         quantise_adjacency(0, 2)
         spread_dinv(1)
-        group_weights(0, 0, HALF, "scalar")
+        group_weights(0, 0, HALF, "vector")
         group_weights(0, HALF, O, "vector")
 
         for i in range(UNITS + 2):
             b, r = divmod(i, TILES)
             nxt = b + 1
             far = b + 2
-            if nxt >= B and i < UNITS:
-                store_engines = ("vector", "vector")
-            elif r == 1 or i >= UNITS:
+            if nxt >= B:
                 store_engines = ("scalar", "vector")
             else:
                 store_engines = ("scalar", "scalar")
@@ -261,7 +261,7 @@ def tile_gcnconv_pa_kernel(tc, X, W, out):
             if nxt < B:
                 quantise_features(nxt, r * QUARTER, (r + 1) * QUARTER)
             if i == 0:
-                group_weights(1, 0, HALF, "scalar")
+                group_weights(1, 0, HALF, "vector")
             if i + 1 < UNITS:
                 first_product(i + 1, 0)
             if 1 <= i <= UNITS:

@@ -85,13 +85,11 @@ def tile_gcnconv_pa_kernel(tc, X, W, out):
             nc.vector.scalar_tensor_tensor(out=dinv[:], in0=deg[:], scalar=0.0, in1=recip[:], op0=ALU.is_gt, op1=ALU.mult)
 
         def spread_dinv(b):
-            repeated = stage.tile([P, PACK, P], F32, name="repeated")
-            nc.gpsimd.tensor_scalar(out=repeated[:], in0=tiles["dinv", b][:].unsqueeze(2).to_broadcast([P, PACK, P]), scalar1=1.0, scalar2=0.0,
-                                    op0=ALU.mult, op1=ALU.add)
             bank = psum.tile([P, N], F32, name="bank")
             tiles["dinv_bank", b] = bank
             for t in range(PACK):
-                nc.tensor.transpose(out=bank[:, t * P:(t + 1) * P], in_=repeated[:, t, :], identity=ident_f[:])
+                nc.tensor.matmul(out=bank[:, t * P:(t + 1) * P], lhsT=tiles["dinv", b][:, t:t + 1].to_broadcast([P, P]), rhs=ident_f[:],
+                                 start=True, stop=True)
 
         def fetch_dinv_row(b):
             row = graph.tile([P, N], F32, name="dinv_row")

@@ -118,9 +118,9 @@ def tile_gcnconv_pa_kernel(tc, X, W, out):
             nc.vector.tensor_tensor(out=tiles["a_grp", b][:, r, :, :], in0=tiles["a_bank", b, r][:].rearrange("p t j -> p j t"),
                                     in1=tiles["pair", b][:, :, r * P:(r + 1) * P].rearrange("p t j -> p j t"), op=ALU.mult)
 
-        def quantise_adjacency(b, r):
-            cols = slice(r * P, (r + 1) * P)
-            quantise(tiles["a_code", b][:, cols], tiles["a_scale", b][:, cols], tiles["a_grp", b][:, r, :, :].rearrange("p j t -> p (j t)"))
+        def quantise_adjacency(b, first, last):
+            cols = slice(first * P, last * P)
+            quantise(tiles["a_code", b][:, cols], tiles["a_scale", b][:, cols], tiles["a_grp", b][:, first:last, :, :].rearrange("p r j t -> p (r j t)"))
 
         def group_features(b, lo, hi, engine):
             if ("f_grp", b) not in tiles:
@@ -197,11 +197,9 @@ def tile_gcnconv_pa_kernel(tc, X, W, out):
         invert_roots(0)
         spread_dinv(0)
         transpose_adjacency(0, 0)
-        group_features(0, 0, QUARTER, "vector")
-        group_features(0, QUARTER, 2 * QUARTER, "vector")
-        group_features(0, 2 * QUARTER, 3 * QUARTER, "vector")
+        group_features(0, 0, 2 * QUARTER, "vector")
         fetch_dinv_row(0)
-        group_features(0, 3 * QUARTER, C, "vector")
+        group_features(0, 2 * QUARTER, C, "vector")
         quantise_features(0, 0, 2 * QUARTER)
         pair_factors(0)
         transpose_adjacency(0, 1)
@@ -210,15 +208,14 @@ def tile_gcnconv_pa_kernel(tc, X, W, out):
         scale_adjacency(0, 0)
         transpose_adjacency(0, 3)
         quantise_features(0, 2 * QUARTER, C)
-        quantise_adjacency(0, 0)
+        quantise_adjacency(0, 0, 1)
         first_product(0, 0)
         first_product(0, 1)
         root_degrees(1)
         scale_adjacency(0, 1)
         scale_adjacency(0, 2)
-        quantise_adjacency(0, 1)
+        quantise_adjacency(0, 1, 2)
         invert_roots(1)
-        quantise_adjacency(0, 2)
         spread_dinv(1)
         group_weights(0, 0, HALF, "vector")
         group_weights(0, HALF, O, "vector")
@@ -244,8 +241,8 @@ def tile_gcnconv_pa_kernel(tc, X, W, out):
                 invert_roots(far)
             if i == 0:
                 group_weights(1, HALF, O, "vector")
-            if nxt < B:
-                group_features(nxt, r * QUARTER, (r + 1) * QUARTER, "vector")
+            if r % 2 == 0 and nxt < B:
+                group_features(nxt, r * QUARTER, (r + 2) * QUARTER, "vector")
             if i >= 2:
                 store_output(i - 2, 0, store_engines[0])
                 store_output(i - 2, 1, store_engines[1])
@@ -254,10 +251,10 @@ def tile_gcnconv_pa_kernel(tc, X, W, out):
                 fetch_hidden(i, 1, "scalar")
             if r == 0 and nxt < B:
                 fetch_dinv_row(nxt)
-            if i + 3 < UNITS:
-                quantise_adjacency((i + 3) // TILES, (i + 3) % TILES)
-            if nxt < B:
-                quantise_features(nxt, r * QUARTER, (r + 1) * QUARTER)
+            if r % 2 == 0 and i + 3 < UNITS:
+                quantise_adjacency((i + 3) // TILES, (i + 2) % TILES, (i + 3) % TILES + 1)
+            if r % 2 == 1 and nxt < B:
+                quantise_features(nxt, (r - 1) * QUARTER, (r + 1) * QUARTER)
             if i == 0:
                 group_weights(1, 0, HALF, "vector")
             if i + 1 < UNITS:

from contextlib import ExitStack

import concourse.mybir as mybir
from concourse.masks import make_identity

B, N, C, O = 4, 512, 1024, 1024
FLOPS = 2 * B * N * N * C + 2 * B * N * C * O

FP8X4 = mybir.dt.float8_e4m3fn_x4
BF16 = mybir.dt.bfloat16
F32 = mybir.dt.float32
U32 = mybir.dt.uint32
U8 = mybir.dt.uint8
ALU = mybir.AluOpType
ACT = mybir.ActivationFunctionType

P = 128
PACK = 4
TILES = N // P
UNITS = B * TILES
HALF = 512
QUARTER = C // 4


def tile_gcnconv_pa_kernel(tc, X, W, out):
    nc = tc.nc
    with ExitStack() as ctx:
        keep = ctx.enter_context(tc.tile_pool(name="keep", bufs=1))
        graph = ctx.enter_context(tc.tile_pool(name="graph", bufs=B))
        stage = ctx.enter_context(tc.tile_pool(name="stage", bufs=2))
        psum = ctx.enter_context(tc.psum_pool(name="psum", bufs=8))

        ident_bf = keep.tile([P, P], BF16, name="ident_bf")
        ident_f = keep.tile([P, P], F32, name="ident_f")
        one = keep.tile([P, 1], F32, name="one")
        unused = keep.tile([P, N], BF16, name="unused")
        x_sb = [keep.tile([P, PACK, N + C], BF16, name="x_sb%d" % b) for b in range(B)]
        w_sb = keep.tile([P, 2 * PACK, O], BF16, name="w_sb")
        w_grp = keep.tile([P, 2, O, PACK], BF16, name="w_grp", align_bytes=64)
        w_code = keep.tile([P, 2, O], U32, name="w_code", align_bytes=64)
        w_scale = keep.tile([P, 2, O], U8, name="w_scale", align_bytes=64)
        tiles = {}

        x_view = X.rearrange("b (t p) w -> b p t w", p=P)
        w_view = W.rearrange("(j p) o -> p j o", p=P)

        def load_x(b, lo, hi, first=0, last=PACK):
            nc.sync.dma_start(out=x_sb[b][:, first:last, lo:hi], in_=x_view[b][:, first:last, lo:hi])

        def load_w(s):
            rows = slice(PACK * s, PACK * s + PACK)
            nc.sync.dma_start(out=w_sb[:, rows, :], in_=w_view[:, rows, :])

        def copy_on(engine, dst, src):
            if engine == "vector":
                nc.vector.tensor_copy(out=dst, in_=src)
            else:
                nc.scalar.copy(out=dst, in_=src)

        def group(engine, dst, src):
            copy_on(engine, dst.rearrange("p (c i) t -> p c t i", i=4), src.rearrange("p t (c i) -> p c t i", i=4))

        def quantise(code, scale, grouped):
            nc.vector.quantize_mx(out=code.bitcast(FP8X4), scales=scale, in_=grouped)

        def degrees(b, first, last):
            if first == 0:
                tiles["deg", b] = graph.tile([P, PACK], F32, name="deg")
            for t in range(first, last):
                nc.scalar.activation(out=unused[:], in_=x_sb[b][:, t, 0:N], func=ACT.Copy, accum_out=tiles["deg", b][:, t:t + 1])

        def root_degrees(b):
            root = graph.tile([P, PACK], F32, name="root")
            tiles["root", b] = root
            nc.scalar.activation(out=root[:], in_=tiles["deg", b][:], func=ACT.Sqrt)

        def invert_roots(b):
            deg = tiles["deg", b]
            safe = graph.tile([P, PACK], F32, name="safe")
            recip = graph.tile([P, PACK], F32, name="recip")
            dinv = graph.tile([P, PACK], F32, name="dinv")
            tiles["dinv", b] = dinv
            nc.vector.scalar_tensor_tensor(out=safe[:], in0=deg[:], scalar=0.0, in1=tiles["root", b][:], op0=ALU.is_le, op1=ALU.max)
            nc.vector.reciprocal(out=recip[:], in_=safe[:])
            nc.vector.scalar_tensor_tensor(out=dinv[:], in0=deg[:], scalar=0.0, in1=recip[:], op0=ALU.is_gt, op1=ALU.mult)

        def spread_dinv(b):
            bank = psum.tile([P, N], F32, name="bank")
            tiles["dinv_bank", b] = bank
            for t in range(PACK):
                nc.tensor.matmul(out=bank[:, t * P:(t + 1) * P], lhsT=tiles["dinv", b][:, t:t + 1].to_broadcast([P, P]), rhs=ident_f[:],
                                 start=True, stop=True)

        def fetch_dinv_row(b):
            row = graph.tile([P, N], F32, name="dinv_row")
            tiles["dinv_row", b] = row
            nc.scalar.copy(out=row[:], in_=tiles["dinv_bank", b][:])

        def pair_factors(b):
            pair = stage.tile([P, PACK, N], F32, name="pair")
            tiles["pair", b] = pair
            for t in range(PACK):
                nc.vector.tensor_scalar(out=pair[:, t, :], in0=tiles["dinv_row", b][:], scalar1=tiles["dinv", b][:, t:t + 1], scalar2=None, op0=ALU.mult)

        def transpose_adjacency(b, r):
            bank = psum.tile([P, PACK, P], F32, name="bank")
            tiles["a_bank", b, r] = bank
            for t in range(PACK):
                nc.tensor.matmul(out=bank[:, t, :], lhsT=x_sb[b][:, r, t * P:(t + 1) * P], rhs=ident_bf[:], start=True, stop=(t != r))
                if t == r:
                    nc.tensor.matmul(out=bank[:, t, :], lhsT=ident_bf[:], rhs=ident_bf[:], start=False, stop=True)

        def scale_adjacency(b, r):
            if ("a_grp", b) not in tiles:
                tiles["a_grp", b] = graph.tile([P, TILES, P, PACK], BF16, name="a_grp", align_bytes=64)
                tiles["a_code", b] = graph.tile([P, N], U32, name="a_code", align_bytes=64)
                tiles["a_scale", b] = graph.tile([P, N], U8, name="a_scale", align_bytes=64)
            nc.vector.tensor_tensor(out=tiles["a_grp", b][:, r, :, :], in0=tiles["a_bank", b, r][:].rearrange("p t j -> p j t"),
                                    in1=tiles["pair", b][:, :, r * P:(r + 1) * P].rearrange("p t j -> p j t"), op=ALU.mult)

        def quantise_adjacency(b, first, last):
            cols = slice(first * P, last * P)
            quantise(tiles["a_code", b][:, cols], tiles["a_scale", b][:, cols], tiles["a_grp", b][:, first:last, :, :].rearrange("p r j t -> p (r j t)"))

        def group_features(b, lo, hi, engine):
            if ("f_grp", b) not in tiles:
                tiles["f_grp", b] = stage.tile([P, C, PACK], BF16, name="f_grp", align_bytes=64)
                tiles["f_code", b] = graph.tile([P, C], U32, name="f_code", align_bytes=64)
                tiles["f_scale", b] = graph.tile([P, C], U8, name="f_scale", align_bytes=64)
            group(engine, tiles["f_grp", b][:, lo:hi, :], x_sb[b][:, :, N + lo:N + hi])

        def quantise_features(b, lo, hi):
            quantise(tiles["f_code", b][:, lo:hi], tiles["f_scale", b][:, lo:hi], tiles["f_grp", b][:, lo:hi, :].rearrange("p c t -> p (c t)"))

        def group_weights(s, lo, hi, engine):
            group(engine, w_grp[:, s, lo:hi, :], w_sb[:, PACK * s:PACK * s + PACK, lo:hi])

        def quantise_weights(s):
            quantise(w_code[:, s, :], w_scale[:, s, :], w_grp[:, s, :, :].rearrange("p o t -> p (o t)"))

        def first_product(u, s):
            b, r = divmod(u, TILES)
            bank = psum.tile([P, PACK, P], F32, name="bank")
            tiles["h_bank", u, s] = bank
            nodes = slice(r * P, (r + 1) * P)
            for t in range(PACK):
                feats = slice((PACK * s + t) * P, (PACK * s + t + 1) * P)
                nc.tensor.matmul_mx(out=bank[:, t, :], lhsT=tiles["f_code", b][:, feats].bitcast(FP8X4), lhsT_scale=tiles["f_scale", b][:, feats],
                                    rhs=tiles["a_code", b][:, nodes].bitcast(FP8X4), rhs_scale=tiles["a_scale", b][:, nodes], start=True, stop=True)

        def fetch_hidden(u, s, engine):
            if s == 0:
                tiles["h_grp", u] = stage.tile([P, 2, P, PACK], BF16, name="h_grp", bufs=4, align_bytes=64)
            copy_on(engine, tiles["h_grp", u][:, s, :, :], tiles["h_bank", u, s][:].rearrange("p t j -> p j t"))

        def quantise_hidden(u):
            tiles["h_code", u] = stage.tile([P, 2 * P], U32, name="h_code", bufs=4, align_bytes=64)
            tiles["h_scale", u] = stage.tile([P, 2 * P], U8, name="h_scale", bufs=4, align_bytes=64)
            quantise(tiles["h_code", u][:], tiles["h_scale", u][:], tiles["h_grp", u][:].rearrange("p s j t -> p (s j t)"))

        def second_product(u, half):
            bank = psum.tile([P, HALF], F32, name="bank")
            tiles["o_bank", u, half] = bank
            cols = slice(half * HALF, (half + 1) * HALF)
            for s in range(2):
                nodes = slice(s * P, (s + 1) * P)
                nc.tensor.matmul_mx(out=bank[:], lhsT=tiles["h_code", u][:, nodes].bitcast(FP8X4), lhsT_scale=tiles["h_scale", u][:, nodes],
                                    rhs=w_code[:, s, cols].bitcast(FP8X4), rhs_scale=w_scale[:, s, cols], start=(s == 0), stop=(s == 1))

        def store_output(u, half, engine):
            b, r = divmod(u, TILES)
            o_sb = stage.tile([P, HALF], F32, name="o_sb", bufs=8)
            if engine == "vector":
                nc.vector.tensor_scalar_max(out=o_sb[:], in0=tiles["o_bank", u, half][:], scalar1=0.0)
            else:
                nc.scalar.activation(out=o_sb[:], in_=tiles["o_bank", u, half][:], func=ACT.Relu)
            nc.sync.dma_start(out=out[b, r * P:(r + 1) * P, half * HALF:(half + 1) * HALF], in_=o_sb[:])

        load_x(0, 0, N, 0, 2)
        load_x(0, 0, N, 2, PACK)
        load_x(0, N, N + C)
        load_x(1, 0, N)
        load_w(0)
        load_w(1)
        load_x(1, N, N + C)
        load_x(2, 0, N)
        load_x(3, 0, N)
        load_x(2, N, N + C)
        load_x(3, N, N + C)
        make_identity(nc, ident_bf[:])
        make_identity(nc, ident_f[:])
        nc.vector.memset(one[:], 1.0)
        nc.scalar.activation(out=one[:], in_=one[:], func=ACT.Sqrt)

        degrees(0, 0, PACK)
        root_degrees(0)
        invert_roots(0)
        spread_dinv(0)
        transpose_adjacency(0, 0)
        group_features(0, 0, 2 * QUARTER, "vector")
        fetch_dinv_row(0)
        group_features(0, 2 * QUARTER, C, "vector")
        quantise_features(0, 0, 2 * QUARTER)
        pair_factors(0)
        transpose_adjacency(0, 1)
        transpose_adjacency(0, 2)
        degrees(1, 0, PACK)
        scale_adjacency(0, 0)
        transpose_adjacency(0, 3)
        quantise_features(0, 2 * QUARTER, C)
        quantise_adjacency(0, 0, 1)
        first_product(0, 0)
        first_product(0, 1)
        root_degrees(1)
        scale_adjacency(0, 1)
        scale_adjacency(0, 2)
        quantise_adjacency(0, 1, 2)
        invert_roots(1)
        spread_dinv(1)
        group_weights(0, 0, HALF, "vector")
        group_weights(0, HALF, O, "vector")

        for i in range(UNITS + 2):
            b, r = divmod(i, TILES)
            nxt = b + 1
            far = b + 2
            if nxt >= B:
                store_engines = ("scalar", "vector")
            else:
                store_engines = ("scalar", "scalar")

            if TILES <= i + 4 < UNITS:
                transpose_adjacency((i + 4) // TILES, (i + 4) % TILES)
            if i + 3 < UNITS:
                scale_adjacency((i + 3) // TILES, (i + 3) % TILES)
            if 1 <= i <= UNITS:
                quantise_hidden(i - 1)
            if i < 2:
                quantise_weights(i)
            if r == 3 and far < B:
                invert_roots(far)
            if i == 0:
                group_weights(1, HALF, O, "vector")
            if r % 2 == 0 and nxt < B:
                group_features(nxt, r * QUARTER, (r + 2) * QUARTER, "vector")
            if i >= 2:
                store_output(i - 2, 0, store_engines[0])
                store_output(i - 2, 1, store_engines[1])
            if i < UNITS:
                fetch_hidden(i, 0, "scalar")
                fetch_hidden(i, 1, "scalar")
            if r == 0 and nxt < B:
                fetch_dinv_row(nxt)
            if r % 2 == 0 and i + 3 < UNITS:
                quantise_adjacency((i + 3) // TILES, (i + 2) % TILES, (i + 3) % TILES + 1)
            if r % 2 == 1 and nxt < B:
                quantise_features(nxt, (r - 1) * QUARTER, (r + 1) * QUARTER)
            if i == 0:
                group_weights(1, 0, HALF, "vector")
            if i + 1 < UNITS:
                first_product(i + 1, 0)
            if 1 <= i <= UNITS:
                second_product(i - 1, 0)
                second_product(i - 1, 1)
            if i + 1 < UNITS:
                first_product(i + 1, 1)
            if r == 3 and far < B:
                spread_dinv(far)
            if r == 0 and nxt < B:
                pair_factors(nxt)
            if r < 2 and far < B:
                degrees(far, 2 * r, 2 * r + 2)
            if r == 1 and far < B:
                root_degrees(far)
